import numpy as np
import ml_dtypes


BF16 = ml_dtypes.bfloat16


def bf(x):
    return np.asarray(x, np.float32).astype(BF16)


def f64(x):
    return np.asarray(x).astype(np.float64)


E2M1 = np.array([0.0, 0.5, 1.0, 1.5, 2.0, 3.0, 4.0, 6.0, -0.0, -0.5, -1.0, -1.5, -2.0, -3.0, -4.0, -6.0])


def pack_weight(w, fmt):
    k, n = w.shape
    w = f64(bf(w)).reshape(k // 32, 32, n)
    amax = np.abs(w).max(1)
    if fmt == "e4m3":
        byte = np.frexp(amax)[1] - 1 + 127 - 7
    else:
        mant, ex = np.frexp(amax / 6.0)
        byte = np.where(mant > 0.5, ex, ex - 1) + 127
    byte = np.clip(np.where(amax > 0, byte, 1), 1, 254)
    scaled = (w * np.exp2(127.0 - byte)[:, None, :]).reshape(k, n).astype(np.float32)
    by_word = np.ascontiguousarray(scaled.reshape(k // 512, 128, 4, n).transpose(0, 1, 3, 2))
    if fmt == "e4m3":
        words = by_word.astype(ml_dtypes.float8_e4m3fn).view(np.uint8)
    else:
        c = by_word.astype(ml_dtypes.float4_e2m1fn).view(np.uint8) & 0xF
        words = c[..., 0::2] | (c[..., 1::2] << 4)
    return np.ascontiguousarray(words), np.ascontiguousarray(byte.astype(np.uint8).reshape(k // 512, 16, n))


def unpack_weight(words, scales, fmt):
    g, p, n, _ = words.shape
    if fmt == "e4m3":
        vals = np.ascontiguousarray(words).view(ml_dtypes.float8_e4m3fn).astype(np.float64)
    else:
        nib = np.empty((g, p, n, 4), np.uint8)
        nib[..., 0::2] = words & 0xF
        nib[..., 1::2] = words >> 4
        vals = E2M1[nib]
    vals = vals * np.repeat(np.exp2(scales.astype(np.float64) - 127.0), 8, axis=1)[..., None]
    return vals.transpose(0, 1, 3, 2).reshape(g * 512, n)

def pack4(w):
    words, scales = pack_weight(w, "e2m1")
    return words.reshape(words.shape[0], 128, -1), scales


def unpack4(words, scales):
    return unpack_weight(words.reshape(words.shape[0], 128, -1, 2), scales, "e2m1")


def kspread(k):
    return np.exp2(np.repeat(np.random.randint(-6, 7, k // 32), 32).astype(np.float64))


B, S, H, D = 3, 128, 12, 384
DIM = H * D
EPS = 1e-6
QK_RMS = 0.004


def rmsnorm(x, w):
    var = np.mean(x * x, axis=-1, keepdims=True)
    return x * (1.0 / np.sqrt(var + EPS)) * w


def apply_rope(x, freqs_cis):
    x_ = x.reshape(B, H, S, D // 2, 1, 2)
    out = freqs_cis[..., 0] * x_[..., 0] + freqs_cis[..., 1] * x_[..., 1]
    return out.reshape(B, H, S, D)


def heads(t):
    return t.reshape(B, S, H, D).transpose(0, 2, 1, 3)


def setup_inputs():
    s = kspread(DIM)
    col = np.repeat(np.array([QK_RMS, QK_RMS, 1.0]), DIM)
    hidden_states = np.random.standard_normal((B, S, DIM)) * s
    hidden_states_words, hidden_states_scales = pack4(hidden_states.reshape(B * S, DIM).T)
    image_rotary_emb = bf(np.random.standard_normal((1, 1, S, D // 2, 2, 2)))
    words, scales = pack4(np.random.standard_normal((DIM, 3 * DIM)) * col / np.sqrt(DIM) / s[:, None])
    return {"hidden_states_words": hidden_states_words,
            "hidden_states_scales": hidden_states_scales,
            "image_rotary_emb": image_rotary_emb,
            "w_qkv_words": words,
            "w_qkv_scales": scales,
            "b_qkv": bf(np.random.standard_normal(3 * DIM) * 0.5 * col),
            "norm_q_w": bf(1.0 + 0.1 * np.random.standard_normal(D)),
            "norm_k_w": bf(1.0 + 0.1 * np.random.standard_normal(D))}


def reference(hidden_states_words, hidden_states_scales, image_rotary_emb, w_qkv_words, w_qkv_scales, b_qkv, norm_q_w, norm_k_w):
    xq = unpack4(hidden_states_words, hidden_states_scales).T.reshape(B, S, DIM)
    w = unpack4(w_qkv_words, w_qkv_scales).reshape(DIM, 3, DIM)
    b = f64(b_qkv).reshape(3, DIM)
    f = f64(image_rotary_emb)
    q = heads((xq @ w[:, 0]) + b[0])
    k = heads((xq @ w[:, 1]) + b[1])
    v = heads((xq @ w[:, 2]) + b[2])
    q = apply_rope(rmsnorm(q, f64(norm_q_w)), f)
    k = apply_rope(rmsnorm(k, f64(norm_k_w)), f)
    return q, k, v

@@ -1,0 +1,254 @@
+from contextlib import ExitStack
+
+import concourse.mybir as mybir
+
+B, S, H, D = 3, 128, 12, 384
+DIM = H * D
+EPS = 1e-6
+TOKENS = B * S
+FLOPS = 2 * TOKENS * DIM * 3 * DIM
+
+P = 128
+K_PASS = 512
+PASSES = DIM // K_PASS
+BANK = 512
+WIDE = 4 * D
+NARROW = 2 * D
+SETS = 3
+
+F32 = mybir.dt.float32
+BF16 = mybir.dt.bfloat16
+I32 = mybir.dt.int32
+U8 = mybir.dt.uint8
+FP4X4 = mybir.dt.float4_e2m1fn_x4
+ALU = mybir.AluOpType
+ACT = mybir.ActivationFunctionType
+
+Q_COLS, K_COLS, V_COLS = 0, 1, 2
+BLOCKS = (
+    [(V_COLS, 0, NARROW)]
+    + [(Q_COLS, i * WIDE, WIDE) for i in range(3)]
+    + [(V_COLS, NARROW, WIDE)]
+    + [(K_COLS, i * WIDE, WIDE) for i in range(3)]
+    + [(V_COLS, NARROW + WIDE, WIDE), (V_COLS, NARROW + 2 * WIDE, NARROW)]
+)
+
+
+def bank_slices(width):
+    return [slice(n, min(n + BANK, width)) for n in range(0, width, BANK)]
+
+
+def by_pass(flat, width):
+    return flat[:, 0 : PASSES * width].rearrange("p (g n) -> p g n", g=PASSES)
+
+
+def tile_fluxsingleattention_pa_kernel(
+    tc, x_words, x_scales, rope, w_words, w_scales, b_qkv, norm_q_w, norm_k_w, out_q, out_k, out_v
+):
+    nc = tc.nc
+    outs = {Q_COLS: out_q, K_COLS: out_k, V_COLS: out_v}
+
+    with ExitStack() as ctx:
+        keep = ctx.enter_context(tc.tile_pool(name="keep", bufs=1))
+        work = ctx.enter_context(tc.tile_pool(name="work", bufs=2))
+        psum = ctx.enter_context(tc.psum_pool(name="psum", bufs=8))
+        ctx.enter_context(tc.manual_schedule())
+
+        x_codes = keep.tile([P, PASSES, 2 * TOKENS], U8, name="x_codes", align_bytes=64)
+        x_planes = keep.tile([P, PASSES, TOKENS], U8, name="x_planes", align_bytes=64)
+        w_codes = [keep.tile([P, PASSES * 2 * WIDE], U8, name="w_codes%d" % i, align_bytes=64) for i in range(SETS)]
+        w_planes = [keep.tile([P, PASSES * WIDE], U8, name="w_planes%d" % i, align_bytes=64) for i in range(SETS)]
+        bias = keep.tile([P, 3 * DIM], BF16, name="bias", align_bytes=64)
+        rope_in = keep.tile([P, 2 * D], BF16, name="rope_in", align_bytes=64)
+        rows = keep.tile([P, 2 * D + NARROW], BF16, name="rows", align_bytes=64)
+        ones = keep.tile([P, P], BF16, name="ones", align_bytes=64)
+        warm = keep.tile([P, 1], F32, name="warm", align_bytes=64)
+        gains = {t: keep.tile([P, 2, D], F32, name="gain%d" % t, align_bytes=64) for t in (Q_COLS, K_COLS)}
+
+        def load_codes(n, first, last):
+            t, c0, width = BLOCKS[n]
+            col = 2 * (t * DIM + c0)
+            dst = by_pass(w_codes[n % SETS], 2 * width)
+            nc.sync.dma_start(
+                out=dst[:, first:last, :].bitcast(I32),
+                in_=w_words[first:last, :, col : col + 2 * width].rearrange("g p n -> p g n").bitcast(I32),
+            )
+
+        def load_scales(n):
+            t, c0, width = BLOCKS[n]
+            col = t * DIM + c0
+            dst = by_pass(w_planes[n % SETS], width)
+            for quad in range(4):
+                nc.sync.dma_start(
+                    out=dst[32 * quad : 32 * quad + 4, :, :].bitcast(I32),
+                    in_=w_scales[:, 4 * quad : 4 * quad + 4, col : col + width].rearrange("g r n -> r g n").bitcast(I32),
+                )
+
+        def load_bias(n):
+            t, c0, width = BLOCKS[n]
+            cols = slice(t * DIM + c0, t * DIM + c0 + width)
+            nc.sync.dma_start(out=bias[:, cols], in_=b_qkv[cols].partition_broadcast(P))
+
+        def load_x_codes(first, last):
+            nc.sync.dma_start(
+                out=x_codes[:, first:last, :].bitcast(I32),
+                in_=x_words[first:last].rearrange("g p n -> p g n").bitcast(I32),
+            )
+
+        def load_block(n):
+            load_codes(n, 0, 3)
+            load_scales(n)
+            load_codes(n, 3, 6)
+            load_bias(n)
+            load_codes(n, 6, 9)
+
+        def multiply(acc, n, batch, cols, g):
+            width = BLOCKS[n][2]
+            codes = by_pass(w_codes[n % SETS], 2 * width)
+            planes = by_pass(w_planes[n % SETS], width)
+            tokens = slice(batch * S, (batch + 1) * S)
+            nc.tensor.matmul_mx(
+                out=acc[:, 0 : cols.stop - cols.start],
+                lhsT=x_codes[:, g, 2 * tokens.start : 2 * tokens.stop].bitcast(FP4X4),
+                lhsT_scale=x_planes[:, g, tokens],
+                rhs=codes[:, g, 2 * cols.start : 2 * cols.stop].bitcast(FP4X4),
+                rhs_scale=planes[:, g, cols],
+                start=(g == 0),
+                stop=(g == PASSES - 1),
+            )
+
+        def add_bias(dst, acc, n, cols):
+            t, c0, width = BLOCKS[n]
+            base = t * DIM + c0
+            nc.vector.tensor_tensor(
+                out=dst[:, cols],
+                in0=acc[:, 0 : cols.stop - cols.start],
+                in1=bias[:, base + cols.start : base + cols.stop],
+                op=ALU.add,
+            )
+
+        def store(n, batch, result):
+            t, c0, width = BLOCKS[n]
+            heads = width // D
+            nc.gpsimd.dma_start(
+                out=outs[t][batch, c0 // D : c0 // D + heads, :, :].rearrange("h s d -> s h d"),
+                in_=result[:, 0:width].rearrange("p (h d) -> p h d", d=D),
+            )
+
+        def norm_and_rope(n, batch, biased):
+            t = BLOCKS[n][0]
+            gain = gains[t]
+            ssq = work.tile([P, 4], F32, name="ssq", bufs=3)
+            std = work.tile([P, 4], F32, name="std", bufs=3)
+            rstd = work.tile([P, 4], F32, name="rstd", bufs=3)
+            for h in range(4):
+                junk = work.tile([P, D], F32, name="junk")
+                nc.scalar.activation(
+                    out=junk[:], in_=biased[:, h * D : (h + 1) * D], func=ACT.Square, accum_out=ssq[:, h : h + 1]
+                )
+            nc.scalar.activation(out=std[:], in_=ssq[:], func=ACT.Sqrt, bias=D * EPS)
+            halves = []
+            pairs = biased[:].rearrange("p (h j c) -> p h j c", h=4, c=2)
+            for c in range(2):
+                half = work.tile([P, WIDE], F32, name="half%d" % c, bufs=1)
+                nc.vector.tensor_tensor(
+                    out=half[:].rearrange("p (h j i) -> p h j i", h=4, i=2),
+                    in0=pairs[:, :, :, c : c + 1].to_broadcast([P, 4, D // 2, 2]),
+                    in1=gain[:, c, :].rearrange("p (j i) -> p j i", i=2).unsqueeze(1).to_broadcast([P, 4, D // 2, 2]),
+                    op=ALU.mult,
+                )
+                halves.append(half)
+            nc.vector.reciprocal(out=rstd[:], in_=std[:])
+            result = work.tile([P, WIDE], F32, name="result", bufs=4)
+            nc.vector.tensor_tensor(out=result[:], in0=halves[0][:], in1=halves[1][:], op=ALU.add)
+            for h in range(4):
+                cols = slice(h * D, (h + 1) * D)
+                nc.scalar.activation(out=result[:, cols], in_=result[:, cols], func=ACT.Copy, scale=rstd[:, h : h + 1])
+            return result
+
+        nc.vector.memset(x_planes[:].rearrange("p g n -> p (g n)").bitcast(I32), 0)
+        nc.vector.memset(w_planes[0][:, 0 : PASSES * NARROW].bitcast(I32), 0)
+        nc.gpsimd.memset(rows[:], 0.0)
+        nc.gpsimd.memset(ones[:], 1.0)
+        nc.gpsimd.dma_start(out=rows[0:1, 0:D], in_=norm_q_w.unsqueeze(0))
+        nc.gpsimd.dma_start(out=rows[0:1, D : 2 * D], in_=norm_k_w.unsqueeze(0))
+        nc.gpsimd.dma_start(out=rows[0:1, 2 * D : 2 * D + NARROW], in_=b_qkv[2 * DIM : 2 * DIM + NARROW].unsqueeze(0))
+        nc.gpsimd.dma_start(out=rope_in[:], in_=rope.rearrange("a b s j i c -> (a b s) (j i c)"))
+        nc.gpsimd.memset(w_planes[1][:].bitcast(I32), 0)
+        nc.gpsimd.memset(w_planes[2][:].bitcast(I32), 0)
+        nc.gpsimd.memset(w_planes[0][:, PASSES * NARROW : PASSES * WIDE].bitcast(I32), 0)
+        nc.vector.memset(warm[:], 1.0)
+        nc.scalar.activation(out=warm[:], in_=warm[:], func=ACT.Sqrt)
+
+        load_x_codes(0, 1)
+        load_codes(0, 0, 1)
+        for quad in range(4):
+            nc.sync.dma_start(
+                out=x_planes[32 * quad : 32 * quad + 4, :, :].bitcast(I32),
+                in_=x_scales[:, 4 * quad : 4 * quad + 4, :].rearrange("g r n -> r g n").bitcast(I32),
+            )
+        load_scales(0)
+        load_x_codes(1, 3)
+        load_codes(0, 1, 3)
+        load_x_codes(3, 9)
+        load_codes(0, 3, 6)
+        load_codes(0, 6, 9)
+        load_block(1)
+        load_block(2)
+
+        accs = {}
+        for batch in range(B):
+            for i in range(2):
+                acc = psum.tile([P, BANK], F32, name="acc")
+                accs[batch, i] = acc
+        for g in range(PASSES):
+            for batch in range(B):
+                for i, cols in enumerate(bank_slices(NARROW)):
+                    multiply(accs[batch, i], 0, batch, cols, g)
+            if g == 1:
+                spread = []
+                for cols in (slice(0, D), slice(D, 2 * D)):
+                    acc = psum.tile([P, BANK], F32, name="acc")
+                    nc.tensor.matmul(out=acc[:, 0:D], lhsT=ones[:], rhs=rows[:, cols], start=True, stop=True)
+                    spread.append(acc)
+                for t in (Q_COLS, K_COLS):
+                    for c in range(2):
+                        nc.vector.scalar_tensor_tensor(
+                            out=gains[t][:, c, :].rearrange("p (j i) -> p j i", i=2),
+                            in0=rope_in[:].rearrange("p (j i c) -> p j i c", i=2, c=2)[:, :, :, c],
+                            scalar=float(D) ** 0.5,
+                            in1=spread[t][:, 0:D].rearrange("p (j c) -> p j c", c=2)[:, :, c : c + 1].to_broadcast([P, D // 2, 2]),
+                            op0=ALU.mult,
+                            op1=ALU.mult,
+                        )
+            if g == 4:
+                for cols in bank_slices(NARROW):
+                    acc = psum.tile([P, BANK], F32, name="acc")
+                    n = cols.stop - cols.start
+                    nc.tensor.matmul(
+                        out=acc[:, 0:n], lhsT=ones[:], rhs=rows[:, 2 * D + cols.start : 2 * D + cols.stop], start=True, stop=True
+                    )
+                    nc.scalar.copy(out=bias[:, 2 * DIM + cols.start : 2 * DIM + cols.stop], in_=acc[:, 0:n])
+        for batch in range(B):
+            result = work.tile([P, WIDE], F32, name="result", bufs=4)
+            for i, cols in enumerate(bank_slices(NARROW)):
+                add_bias(result, accs[batch, i], 0, cols)
+            store(0, batch, result)
+
+        for n in range(1, len(BLOCKS)):
+            if n + 2 < len(BLOCKS):
+                load_block(n + 2)
+            t, c0, width = BLOCKS[n]
+            for batch in range(B):
+                if t == V_COLS:
+                    dst = work.tile([P, WIDE], F32, name="result", bufs=4)
+                else:
+                    dst = work.tile([P, WIDE], F32, name="biased")
+                for cols in bank_slices(width):
+                    acc = psum.tile([P, BANK], F32, name="acc")
+                    for g in range(PASSES):
+                        multiply(acc, n, batch, cols, g)
+                    add_bias(dst, acc, n, cols)
+                if t != V_COLS:
+                    dst = norm_and_rope(n, batch, dst)
+                store(n, batch, dst)

@@ -1,6 +1,7 @@
 from contextlib import ExitStack
 
 import concourse.mybir as mybir
+from concourse.masks import make_identity
 
 B, S, H, D = 3, 128, 12, 384
 DIM = H * D
@@ -15,6 +16,9 @@ BANK = 512
 WIDE = 4 * D
 NARROW = 2 * D
 SETS = 3
+BIAS_ROWS = 3 * DIM // BANK
+NORM_ROW = {0: BIAS_ROWS, 1: BIAS_ROWS + 1}
+ALL_ROWS = BIAS_ROWS + 2
 
 F32 = mybir.dt.float32
 BF16 = mybir.dt.bfloat16
@@ -36,6 +40,12 @@ BLOCKS = (
 
 def bank_slices(width):
     return [slice(n, min(n + BANK, width)) for n in range(0, width, BANK)]
+
+
+def bias_rows(block):
+    t, c0, width = block
+    first = t * DIM + c0
+    return list(range(first // BANK, (first + width - 1) // BANK + 1))
 
 
 def by_pass(flat, width):
@@ -60,8 +70,9 @@ def tile_fluxsingleattention_pa_kernel(
         w_planes = [keep.tile([P, PASSES * WIDE], U8, name="w_planes%d" % i, align_bytes=64) for i in range(SETS)]
         bias = keep.tile([P, 3 * DIM], BF16, name="bias", align_bytes=64)
         rope_in = keep.tile([P, 2 * D], BF16, name="rope_in", align_bytes=64)
-        rows = keep.tile([P, 2 * D + NARROW], BF16, name="rows", align_bytes=64)
-        ones = keep.tile([P, P], BF16, name="ones", align_bytes=64)
+        rows = keep.tile([P, BANK], BF16, name="rows", align_bytes=64)
+        ident = keep.tile([P, P], BF16, name="ident", align_bytes=64)
+        pick = keep.tile([P, ALL_ROWS, P], BF16, name="pick", align_bytes=64)
         warm = keep.tile([P, 1], F32, name="warm", align_bytes=64)
         gains = {t: keep.tile([P, 2, D], F32, name="gain%d" % t, align_bytes=64) for t in (Q_COLS, K_COLS)}
 
@@ -74,6 +85,15 @@ def tile_fluxsingleattention_pa_kernel(
                 in_=w_words[first:last, :, col : col + 2 * width].rearrange("g p n -> p g n").bitcast(I32),
             )
 
+        def load_scale_rows(n, r):
+            t, c0, width = BLOCKS[n]
+            col = t * DIM + c0
+            dst = by_pass(w_planes[n % SETS], width)
+            nc.sync.dma_start(
+                out=dst[r:P:32, :, :].bitcast(I32),
+                in_=w_scales[:, r:16:4, col : col + width].rearrange("g r n -> r g n").bitcast(I32),
+            )
+
         def load_scales(n):
             t, c0, width = BLOCKS[n]
             col = t * DIM + c0
@@ -84,10 +104,14 @@ def tile_fluxsingleattention_pa_kernel(
                     in_=w_scales[:, 4 * quad : 4 * quad + 4, col : col + width].rearrange("g r n -> r g n").bitcast(I32),
                 )
 
-        def load_bias(n):
-            t, c0, width = BLOCKS[n]
-            cols = slice(t * DIM + c0, t * DIM + c0 + width)
-            nc.sync.dma_start(out=bias[:, cols], in_=b_qkv[cols].partition_broadcast(P))
+        def spread_row(row, width):
+            acc = psum.tile([P, BANK], F32, name="acc")
+            nc.tensor.matmul(out=acc[:, 0:width], lhsT=pick[:, row, :], rhs=rows[:, 0:width], start=True, stop=True)
+            return acc
+
+        def spread_bias(row):
+            acc = spread_row(row, BANK)
+            nc.scalar.copy(out=bias[:, row * BANK : (row + 1) * BANK], in_=acc[:])
 
         def load_x_codes(first, last):
             nc.sync.dma_start(
@@ -96,11 +120,9 @@ def tile_fluxsingleattention_pa_kernel(
             )
 
         def load_block(n):
-            load_codes(n, 0, 3)
-            load_scales(n)
-            load_codes(n, 3, 6)
-            load_bias(n)
-            load_codes(n, 6, 9)
+            for r, (first, last) in enumerate(((0, 3), (3, 5), (5, 7), (7, 9))):
+                load_scale_rows(n, r)
+                load_codes(n, first, last)
 
         def multiply(acc, n, batch, cols, g):
             width = BLOCKS[n][2]
@@ -134,6 +156,16 @@ def tile_fluxsingleattention_pa_kernel(
                 out=outs[t][batch, c0 // D : c0 // D + heads, :, :].rearrange("h s d -> s h d"),
                 in_=result[:, 0:width].rearrange("p (h d) -> p h d", d=D),
             )
+
+        def store_cols(n, batch, result, cols):
+            t, c0, width = BLOCKS[n]
+            start = cols.start
+            while start < cols.stop:
+                stop = min(cols.stop, start - start % D + D)
+                nc.sync.dma_start(
+                    out=outs[t][batch, (c0 + start) // D, :, start % D : start % D + stop - start], in_=result[:, start:stop]
+                )
+                start = stop
 
         def norm_and_rope(n, batch, biased):
             t = BLOCKS[n][0]
@@ -169,16 +201,20 @@ def tile_fluxsingleattention_pa_kernel(
         nc.vector.memset(x_planes[:].rearrange("p g n -> p (g n)").bitcast(I32), 0)
         nc.vector.memset(w_planes[0][:, 0 : PASSES * NARROW].bitcast(I32), 0)
         nc.gpsimd.memset(rows[:], 0.0)
-        nc.gpsimd.memset(ones[:], 1.0)
-        nc.gpsimd.dma_start(out=rows[0:1, 0:D], in_=norm_q_w.unsqueeze(0))
-        nc.gpsimd.dma_start(out=rows[0:1, D : 2 * D], in_=norm_k_w.unsqueeze(0))
-        nc.gpsimd.dma_start(out=rows[0:1, 2 * D : 2 * D + NARROW], in_=b_qkv[2 * DIM : 2 * DIM + NARROW].unsqueeze(0))
+        nc.gpsimd.dma_start(out=rows[0:BIAS_ROWS, :], in_=b_qkv.rearrange("(r n) -> r n", n=BANK))
+        nc.gpsimd.dma_start(out=rows[BIAS_ROWS : BIAS_ROWS + 1, 0:D], in_=norm_q_w.unsqueeze(0))
+        nc.gpsimd.dma_start(out=rows[BIAS_ROWS + 1 : BIAS_ROWS + 2, 0:D], in_=norm_k_w.unsqueeze(0))
+        make_identity(nc, ident[:])
         nc.gpsimd.dma_start(out=rope_in[:], in_=rope.rearrange("a b s j i c -> (a b s) (j i c)"))
         nc.gpsimd.memset(w_planes[1][:].bitcast(I32), 0)
         nc.gpsimd.memset(w_planes[2][:].bitcast(I32), 0)
         nc.gpsimd.memset(w_planes[0][:, PASSES * NARROW : PASSES * WIDE].bitcast(I32), 0)
         nc.vector.memset(warm[:], 1.0)
         nc.scalar.activation(out=warm[:], in_=warm[:], func=ACT.Sqrt)
+        for first, last in ((18, 20), (27, 29), (0, 9), (9, 18), (20, 27)):
+            nc.scalar.copy(
+                out=pick[:, first:last, :], in_=ident[:, first:last].unsqueeze(2).to_broadcast([P, last - first, P])
+            )
 
         load_x_codes(0, 1)
         load_codes(0, 0, 1)
@@ -201,34 +237,26 @@ def tile_fluxsingleattention_pa_kernel(
             for i in range(2):
                 acc = psum.tile([P, BANK], F32, name="acc")
                 accs[batch, i] = acc
+        spread_bias(18)
+        spread_bias(19)
+        done = [18, 19, 0, 1, 2]
+        for t in (Q_COLS, K_COLS):
+            norm = spread_row(NORM_ROW[t], D)
+            for c in range(2):
+                nc.vector.scalar_tensor_tensor(
+                    out=gains[t][:, c, :].rearrange("p (j i) -> p j i", i=2),
+                    in0=rope_in[:].rearrange("p (j i c) -> p j i c", i=2, c=2)[:, :, :, c],
+                    scalar=float(D) ** 0.5,
+                    in1=norm[:, 0:D].rearrange("p (j c) -> p j c", c=2)[:, :, c : c + 1].to_broadcast([P, D // 2, 2]),
+                    op0=ALU.mult,
+                    op1=ALU.mult,
+                )
         for g in range(PASSES):
             for batch in range(B):
                 for i, cols in enumerate(bank_slices(NARROW)):
                     multiply(accs[batch, i], 0, batch, cols, g)
-            if g == 1:
-                spread = []
-                for cols in (slice(0, D), slice(D, 2 * D)):
-                    acc = psum.tile([P, BANK], F32, name="acc")
-                    nc.tensor.matmul(out=acc[:, 0:D], lhsT=ones[:], rhs=rows[:, cols], start=True, stop=True)
-                    spread.append(acc)
-                for t in (Q_COLS, K_COLS):
-                    for c in range(2):
-                        nc.vector.scalar_tensor_tensor(
-                            out=gains[t][:, c, :].rearrange("p (j i) -> p j i", i=2),
-                            in0=rope_in[:].rearrange("p (j i c) -> p j i c", i=2, c=2)[:, :, :, c],
-                            scalar=float(D) ** 0.5,
-                            in1=spread[t][:, 0:D].rearrange("p (j c) -> p j c", c=2)[:, :, c : c + 1].to_broadcast([P, D // 2, 2]),
-                            op0=ALU.mult,
-                            op1=ALU.mult,
-                        )
-            if g == 4:
-                for cols in bank_slices(NARROW):
-                    acc = psum.tile([P, BANK], F32, name="acc")
-                    n = cols.stop - cols.start
-                    nc.tensor.matmul(
-                        out=acc[:, 0:n], lhsT=ones[:], rhs=rows[:, 2 * D + cols.start : 2 * D + cols.stop], start=True, stop=True
-                    )
-                    nc.scalar.copy(out=bias[:, 2 * DIM + cols.start : 2 * DIM + cols.stop], in_=acc[:, 0:n])
+            if g in (3, 4, 5):
+                spread_bias(g - 3)
         for batch in range(B):
             result = work.tile([P, WIDE], F32, name="result", bufs=4)
             for i, cols in enumerate(bank_slices(NARROW)):
@@ -239,7 +267,12 @@ def tile_fluxsingleattention_pa_kernel(
             if n + 2 < len(BLOCKS):
                 load_block(n + 2)
             t, c0, width = BLOCKS[n]
+            last = n == len(BLOCKS) - 1
+            todo = [r for r in bias_rows(BLOCKS[n + 1]) if r not in done] if n + 1 < len(BLOCKS) else []
+            done.extend(todo)
             for batch in range(B):
+                if batch < len(todo):
+                    spread_bias(todo[batch])
                 if t == V_COLS:
                     dst = work.tile([P, WIDE], F32, name="result", bufs=4)
                 else:
@@ -249,6 +282,9 @@ def tile_fluxsingleattention_pa_kernel(
                     for g in range(PASSES):
                         multiply(acc, n, batch, cols, g)
                     add_bias(dst, acc, n, cols)
+                    if last:
+                        store_cols(n, batch, dst, cols)
                 if t != V_COLS:
                     dst = norm_and_rope(n, batch, dst)
-                store(n, batch, dst)
+                if not last:
+                    store(n, batch, dst)

@@ -1,7 +1,6 @@
 from contextlib import ExitStack
 
 import concourse.mybir as mybir
-from concourse.masks import make_identity
 
 B, S, H, D = 3, 128, 12, 384
 DIM = H * D
@@ -16,9 +15,6 @@ BANK = 512
 WIDE = 4 * D
 NARROW = 2 * D
 SETS = 3
-BIAS_ROWS = 3 * DIM // BANK
-NORM_ROW = {0: BIAS_ROWS, 1: BIAS_ROWS + 1}
-ALL_ROWS = BIAS_ROWS + 2
 
 F32 = mybir.dt.float32
 BF16 = mybir.dt.bfloat16
@@ -42,12 +38,6 @@ def bank_slices(width):
     return [slice(n, min(n + BANK, width)) for n in range(0, width, BANK)]
 
 
-def bias_rows(block):
-    t, c0, width = block
-    first = t * DIM + c0
-    return list(range(first // BANK, (first + width - 1) // BANK + 1))
-
-
 def by_pass(flat, width):
     return flat[:, 0 : PASSES * width].rearrange("p (g n) -> p g n", g=PASSES)
 
@@ -64,15 +54,15 @@ def tile_fluxsingleattention_pa_kernel(
         psum = ctx.enter_context(tc.psum_pool(name="psum", bufs=8))
         ctx.enter_context(tc.manual_schedule())
 
-        x_codes = keep.tile([P, PASSES, 2 * TOKENS], U8, name="x_codes", align_bytes=64)
-        x_planes = keep.tile([P, PASSES, TOKENS], U8, name="x_planes", align_bytes=64)
-        w_codes = [keep.tile([P, PASSES * 2 * WIDE], U8, name="w_codes%d" % i, align_bytes=64) for i in range(SETS)]
-        w_planes = [keep.tile([P, PASSES * WIDE], U8, name="w_planes%d" % i, align_bytes=64) for i in range(SETS)]
+        x_codes = keep.tile([P, PASSES, 2 * TOKENS], U8, name="x_codes", align_bytes=256)
+        x_planes = keep.tile([P, PASSES, TOKENS], U8, name="x_planes", align_bytes=256)
+        w_codes = [keep.tile([P, PASSES * 2 * WIDE], U8, name="w_codes%d" % i, align_bytes=256) for i in range(SETS)]
+        w_planes = [keep.tile([P, PASSES * WIDE], U8, name="w_planes%d" % i, align_bytes=256) for i in range(SETS)]
         bias = keep.tile([P, 3 * DIM], BF16, name="bias", align_bytes=64)
         rope_in = keep.tile([P, 2 * D], BF16, name="rope_in", align_bytes=64)
-        rows = keep.tile([P, BANK], BF16, name="rows", align_bytes=64)
-        ident = keep.tile([P, P], BF16, name="ident", align_bytes=64)
-        pick = keep.tile([P, ALL_ROWS, P], BF16, name="pick", align_bytes=64)
+        rows_a = keep.tile([P, 2 * D + NARROW], BF16, name="rows_a", align_bytes=64)
+        rows_b = keep.tile([P, WIDE], BF16, name="rows_b", align_bytes=64)
+        ones = keep.tile([P, P], BF16, name="ones", align_bytes=64)
         warm = keep.tile([P, 1], F32, name="warm", align_bytes=64)
         gains = {t: keep.tile([P, 2, D], F32, name="gain%d" % t, align_bytes=64) for t in (Q_COLS, K_COLS)}
 
@@ -104,14 +94,21 @@ def tile_fluxsingleattention_pa_kernel(
                     in_=w_scales[:, 4 * quad : 4 * quad + 4, col : col + width].rearrange("g r n -> r g n").bitcast(I32),
                 )
 
-        def spread_row(row, width):
+        def load_bias(n):
+            t, c0, width = BLOCKS[n]
+            cols = slice(t * DIM + c0, t * DIM + c0 + width)
+            nc.sync.dma_start(out=bias[:, cols], in_=b_qkv[cols].partition_broadcast(P))
+
+        def spread(row):
             acc = psum.tile([P, BANK], F32, name="acc")
-            nc.tensor.matmul(out=acc[:, 0:width], lhsT=pick[:, row, :], rhs=rows[:, 0:width], start=True, stop=True)
+            nc.tensor.matmul(out=acc[:, 0 : row.shape[1]], lhsT=ones[:], rhs=row, start=True, stop=True)
             return acc
 
-        def spread_bias(row):
-            acc = spread_row(row, BANK)
-            nc.scalar.copy(out=bias[:, row * BANK : (row + 1) * BANK], in_=acc[:])
+        def spread_bank(n, rows, first, cols):
+            t, c0, width = BLOCKS[n]
+            base = t * DIM + c0
+            acc = spread(rows[:, first + cols.start : first + cols.stop])
+            nc.scalar.copy(out=bias[:, base + cols.start : base + cols.stop], in_=acc[:, 0 : cols.stop - cols.start])
 
         def load_x_codes(first, last):
             nc.sync.dma_start(
@@ -123,6 +120,8 @@ def tile_fluxsingleattention_pa_kernel(
             for r, (first, last) in enumerate(((0, 3), (3, 5), (5, 7), (7, 9))):
                 load_scale_rows(n, r)
                 load_codes(n, first, last)
+                if r == 1 and n > 1:
+                    load_bias(n)
 
         def multiply(acc, n, batch, cols, g):
             width = BLOCKS[n][2]
@@ -198,23 +197,21 @@ def tile_fluxsingleattention_pa_kernel(
                 nc.scalar.activation(out=result[:, cols], in_=result[:, cols], func=ACT.Copy, scale=rstd[:, h : h + 1])
             return result
 
-        nc.vector.memset(x_planes[:].rearrange("p g n -> p (g n)").bitcast(I32), 0)
+        nc.gpsimd.memset(x_planes[:].rearrange("p g n -> p (g n)").bitcast(I32), 0)
+        nc.gpsimd.memset(rows_a[:].bitcast(I32), 0)
         nc.vector.memset(w_planes[0][:, 0 : PASSES * NARROW].bitcast(I32), 0)
-        nc.gpsimd.memset(rows[:], 0.0)
-        nc.gpsimd.dma_start(out=rows[0:BIAS_ROWS, :], in_=b_qkv.rearrange("(r n) -> r n", n=BANK))
-        nc.gpsimd.dma_start(out=rows[BIAS_ROWS : BIAS_ROWS + 1, 0:D], in_=norm_q_w.unsqueeze(0))
-        nc.gpsimd.dma_start(out=rows[BIAS_ROWS + 1 : BIAS_ROWS + 2, 0:D], in_=norm_k_w.unsqueeze(0))
-        make_identity(nc, ident[:])
+        nc.vector.memset(ones[:], 1.0)
+        nc.vector.memset(warm[:], 1.0)
+        nc.vector.memset(rows_b[:].bitcast(I32), 0)
+        nc.gpsimd.dma_start(out=rows_a[0:1, 2 * D : 2 * D + NARROW], in_=b_qkv[2 * DIM : 2 * DIM + NARROW].unsqueeze(0))
+        nc.gpsimd.dma_start(out=rows_a[0:1, 0:D], in_=norm_q_w.unsqueeze(0))
+        nc.gpsimd.dma_start(out=rows_a[0:1, D : 2 * D], in_=norm_k_w.unsqueeze(0))
         nc.gpsimd.dma_start(out=rope_in[:], in_=rope.rearrange("a b s j i c -> (a b s) (j i c)"))
+        nc.gpsimd.dma_start(out=rows_b[0:1, :], in_=b_qkv[0:WIDE].unsqueeze(0))
         nc.gpsimd.memset(w_planes[1][:].bitcast(I32), 0)
         nc.gpsimd.memset(w_planes[2][:].bitcast(I32), 0)
         nc.gpsimd.memset(w_planes[0][:, PASSES * NARROW : PASSES * WIDE].bitcast(I32), 0)
-        nc.vector.memset(warm[:], 1.0)
         nc.scalar.activation(out=warm[:], in_=warm[:], func=ACT.Sqrt)
-        for first, last in ((18, 20), (27, 29), (0, 9), (9, 18), (20, 27)):
-            nc.scalar.copy(
-                out=pick[:, first:last, :], in_=ident[:, first:last].unsqueeze(2).to_broadcast([P, last - first, P])
-            )
 
         load_x_codes(0, 1)
         load_codes(0, 0, 1)
@@ -237,11 +234,10 @@ def tile_fluxsingleattention_pa_kernel(
             for i in range(2):
                 acc = psum.tile([P, BANK], F32, name="acc")
                 accs[batch, i] = acc
-        spread_bias(18)
-        spread_bias(19)
-        done = [18, 19, 0, 1, 2]
+        for cols in bank_slices(NARROW):
+            spread_bank(0, rows_a, 2 * D, cols)
         for t in (Q_COLS, K_COLS):
-            norm = spread_row(NORM_ROW[t], D)
+            norm = spread(rows_a[:, t * D : (t + 1) * D])
             for c in range(2):
                 nc.vector.scalar_tensor_tensor(
                     out=gains[t][:, c, :].rearrange("p (j i) -> p j i", i=2),
@@ -255,8 +251,8 @@ def tile_fluxsingleattention_pa_kernel(
             for batch in range(B):
                 for i, cols in enumerate(bank_slices(NARROW)):
                     multiply(accs[batch, i], 0, batch, cols, g)
-            if g in (3, 4, 5):
-                spread_bias(g - 3)
+            if g in (4, 5, 6):
+                spread_bank(1, rows_b, 0, bank_slices(WIDE)[g - 4])
         for batch in range(B):
             result = work.tile([P, WIDE], F32, name="result", bufs=4)
             for i, cols in enumerate(bank_slices(NARROW)):
@@ -268,11 +264,7 @@ def tile_fluxsingleattention_pa_kernel(
                 load_block(n + 2)
             t, c0, width = BLOCKS[n]
             last = n == len(BLOCKS) - 1
-            todo = [r for r in bias_rows(BLOCKS[n + 1]) if r not in done] if n + 1 < len(BLOCKS) else []
-            done.extend(todo)
             for batch in range(B):
-                if batch < len(todo):
-                    spread_bias(todo[batch])
                 if t == V_COLS:
                     dst = work.tile([P, WIDE], F32, name="result", bufs=4)
                 else:

from contextlib import ExitStack

import concourse.mybir as mybir

B, S, H, D = 3, 128, 12, 384
DIM = H * D
EPS = 1e-6
TOKENS = B * S
FLOPS = 2 * TOKENS * DIM * 3 * DIM

P = 128
K_PASS = 512
PASSES = DIM // K_PASS
BANK = 512
WIDE = 4 * D
NARROW = 2 * D
SETS = 3

F32 = mybir.dt.float32
BF16 = mybir.dt.bfloat16
I32 = mybir.dt.int32
U8 = mybir.dt.uint8
FP4X4 = mybir.dt.float4_e2m1fn_x4
ALU = mybir.AluOpType
ACT = mybir.ActivationFunctionType

Q_COLS, K_COLS, V_COLS = 0, 1, 2
BLOCKS = (
    [(V_COLS, 0, NARROW)]
    + [(Q_COLS, i * WIDE, WIDE) for i in range(3)]
    + [(V_COLS, NARROW, WIDE)]
    + [(K_COLS, i * WIDE, WIDE) for i in range(3)]
    + [(V_COLS, NARROW + WIDE, WIDE), (V_COLS, NARROW + 2 * WIDE, NARROW)]
)


def bank_slices(width):
    return [slice(n, min(n + BANK, width)) for n in range(0, width, BANK)]


def by_pass(flat, width):
    return flat[:, 0 : PASSES * width].rearrange("p (g n) -> p g n", g=PASSES)


def tile_fluxsingleattention_pa_kernel(
    tc, x_words, x_scales, rope, w_words, w_scales, b_qkv, norm_q_w, norm_k_w, out_q, out_k, out_v
):
    nc = tc.nc
    outs = {Q_COLS: out_q, K_COLS: out_k, V_COLS: out_v}

    with ExitStack() as ctx:
        keep = ctx.enter_context(tc.tile_pool(name="keep", bufs=1))
        work = ctx.enter_context(tc.tile_pool(name="work", bufs=2))
        psum = ctx.enter_context(tc.psum_pool(name="psum", bufs=8))
        ctx.enter_context(tc.manual_schedule())

        x_codes = keep.tile([P, PASSES, 2 * TOKENS], U8, name="x_codes", align_bytes=256)
        x_planes = keep.tile([P, PASSES, TOKENS], U8, name="x_planes", align_bytes=256)
        w_codes = [keep.tile([P, PASSES * 2 * WIDE], U8, name="w_codes%d" % i, align_bytes=256) for i in range(SETS)]
        w_planes = [keep.tile([P, PASSES * WIDE], U8, name="w_planes%d" % i, align_bytes=256) for i in range(SETS)]
        bias = keep.tile([P, 3 * DIM], BF16, name="bias", align_bytes=64)
        rope_in = keep.tile([P, 2 * D], BF16, name="rope_in", align_bytes=64)
        rows_a = keep.tile([P, 2 * D + NARROW], BF16, name="rows_a", align_bytes=64)
        rows_b = keep.tile([P, WIDE], BF16, name="rows_b", align_bytes=64)
        ones = keep.tile([P, P], BF16, name="ones", align_bytes=64)
        warm = keep.tile([P, 1], F32, name="warm", align_bytes=64)
        gains = {t: keep.tile([P, 2, D], F32, name="gain%d" % t, align_bytes=64) for t in (Q_COLS, K_COLS)}

        def load_codes(n, first, last):
            t, c0, width = BLOCKS[n]
            col = 2 * (t * DIM + c0)
            dst = by_pass(w_codes[n % SETS], 2 * width)
            nc.sync.dma_start(
                out=dst[:, first:last, :].bitcast(I32),
                in_=w_words[first:last, :, col : col + 2 * width].rearrange("g p n -> p g n").bitcast(I32),
            )

        def load_scale_rows(n, r):
            t, c0, width = BLOCKS[n]
            col = t * DIM + c0
            dst = by_pass(w_planes[n % SETS], width)
            nc.sync.dma_start(
                out=dst[r:P:32, :, :].bitcast(I32),
                in_=w_scales[:, r:16:4, col : col + width].rearrange("g r n -> r g n").bitcast(I32),
            )

        def load_scales(n):
            t, c0, width = BLOCKS[n]
            col = t * DIM + c0
            dst = by_pass(w_planes[n % SETS], width)
            for quad in range(4):
                nc.sync.dma_start(
                    out=dst[32 * quad : 32 * quad + 4, :, :].bitcast(I32),
                    in_=w_scales[:, 4 * quad : 4 * quad + 4, col : col + width].rearrange("g r n -> r g n").bitcast(I32),
                )

        def load_bias(n):
            t, c0, width = BLOCKS[n]
            cols = slice(t * DIM + c0, t * DIM + c0 + width)
            nc.sync.dma_start(out=bias[:, cols], in_=b_qkv[cols].partition_broadcast(P))

        def spread(row):
            acc = psum.tile([P, BANK], F32, name="acc")
            nc.tensor.matmul(out=acc[:, 0 : row.shape[1]], lhsT=ones[:], rhs=row, start=True, stop=True)
            return acc

        def spread_bank(n, rows, first, cols):
            t, c0, width = BLOCKS[n]
            base = t * DIM + c0
            acc = spread(rows[:, first + cols.start : first + cols.stop])
            nc.scalar.copy(out=bias[:, base + cols.start : base + cols.stop], in_=acc[:, 0 : cols.stop - cols.start])

        def load_x_codes(first, last):
            nc.sync.dma_start(
                out=x_codes[:, first:last, :].bitcast(I32),
                in_=x_words[first:last].rearrange("g p n -> p g n").bitcast(I32),
            )

        def load_block(n):
            for r, (first, last) in enumerate(((0, 3), (3, 5), (5, 7), (7, 9))):
                load_scale_rows(n, r)
                load_codes(n, first, last)
                if r == 1 and n > 1:
                    load_bias(n)

        def multiply(acc, n, batch, cols, g):
            width = BLOCKS[n][2]
            codes = by_pass(w_codes[n % SETS], 2 * width)
            planes = by_pass(w_planes[n % SETS], width)
            tokens = slice(batch * S, (batch + 1) * S)
            nc.tensor.matmul_mx(
                out=acc[:, 0 : cols.stop - cols.start],
                lhsT=x_codes[:, g, 2 * tokens.start : 2 * tokens.stop].bitcast(FP4X4),
                lhsT_scale=x_planes[:, g, tokens],
                rhs=codes[:, g, 2 * cols.start : 2 * cols.stop].bitcast(FP4X4),
                rhs_scale=planes[:, g, cols],
                start=(g == 0),
                stop=(g == PASSES - 1),
            )

        def add_bias(dst, acc, n, cols):
            t, c0, width = BLOCKS[n]
            base = t * DIM + c0
            nc.vector.tensor_tensor(
                out=dst[:, cols],
                in0=acc[:, 0 : cols.stop - cols.start],
                in1=bias[:, base + cols.start : base + cols.stop],
                op=ALU.add,
            )

        def store(n, batch, result):
            t, c0, width = BLOCKS[n]
            heads = width // D
            nc.gpsimd.dma_start(
                out=outs[t][batch, c0 // D : c0 // D + heads, :, :].rearrange("h s d -> s h d"),
                in_=result[:, 0:width].rearrange("p (h d) -> p h d", d=D),
            )

        def store_cols(n, batch, result, cols):
            t, c0, width = BLOCKS[n]
            start = cols.start
            while start < cols.stop:
                stop = min(cols.stop, start - start % D + D)
                nc.sync.dma_start(
                    out=outs[t][batch, (c0 + start) // D, :, start % D : start % D + stop - start], in_=result[:, start:stop]
                )
                start = stop

        def norm_and_rope(n, batch, biased):
            t = BLOCKS[n][0]
            gain = gains[t]
            ssq = work.tile([P, 4], F32, name="ssq", bufs=3)
            std = work.tile([P, 4], F32, name="std", bufs=3)
            rstd = work.tile([P, 4], F32, name="rstd", bufs=3)
            for h in range(4):
                junk = work.tile([P, D], F32, name="junk")
                nc.scalar.activation(
                    out=junk[:], in_=biased[:, h * D : (h + 1) * D], func=ACT.Square, accum_out=ssq[:, h : h + 1]
                )
            nc.scalar.activation(out=std[:], in_=ssq[:], func=ACT.Sqrt, bias=D * EPS)
            halves = []
            pairs = biased[:].rearrange("p (h j c) -> p h j c", h=4, c=2)
            for c in range(2):
                half = work.tile([P, WIDE], F32, name="half%d" % c, bufs=1)
                nc.vector.tensor_tensor(
                    out=half[:].rearrange("p (h j i) -> p h j i", h=4, i=2),
                    in0=pairs[:, :, :, c : c + 1].to_broadcast([P, 4, D // 2, 2]),
                    in1=gain[:, c, :].rearrange("p (j i) -> p j i", i=2).unsqueeze(1).to_broadcast([P, 4, D // 2, 2]),
                    op=ALU.mult,
                )
                halves.append(half)
            nc.vector.reciprocal(out=rstd[:], in_=std[:])
            result = work.tile([P, WIDE], F32, name="result", bufs=4)
            nc.vector.tensor_tensor(out=result[:], in0=halves[0][:], in1=halves[1][:], op=ALU.add)
            for h in range(4):
                cols = slice(h * D, (h + 1) * D)
                nc.scalar.activation(out=result[:, cols], in_=result[:, cols], func=ACT.Copy, scale=rstd[:, h : h + 1])
            return result

        nc.gpsimd.memset(x_planes[:].rearrange("p g n -> p (g n)").bitcast(I32), 0)
        nc.gpsimd.memset(rows_a[:].bitcast(I32), 0)
        nc.vector.memset(w_planes[0][:, 0 : PASSES * NARROW].bitcast(I32), 0)
        nc.vector.memset(ones[:], 1.0)
        nc.vector.memset(warm[:], 1.0)
        nc.vector.memset(rows_b[:].bitcast(I32), 0)
        nc.gpsimd.dma_start(out=rows_a[0:1, 2 * D : 2 * D + NARROW], in_=b_qkv[2 * DIM : 2 * DIM + NARROW].unsqueeze(0))
        nc.gpsimd.dma_start(out=rows_a[0:1, 0:D], in_=norm_q_w.unsqueeze(0))
        nc.gpsimd.dma_start(out=rows_a[0:1, D : 2 * D], in_=norm_k_w.unsqueeze(0))
        nc.gpsimd.dma_start(out=rope_in[:], in_=rope.rearrange("a b s j i c -> (a b s) (j i c)"))
        nc.gpsimd.dma_start(out=rows_b[0:1, :], in_=b_qkv[0:WIDE].unsqueeze(0))
        nc.gpsimd.memset(w_planes[1][:].bitcast(I32), 0)
        nc.gpsimd.memset(w_planes[2][:].bitcast(I32), 0)
        nc.gpsimd.memset(w_planes[0][:, PASSES * NARROW : PASSES * WIDE].bitcast(I32), 0)
        nc.scalar.activation(out=warm[:], in_=warm[:], func=ACT.Sqrt)

        load_x_codes(0, 1)
        load_codes(0, 0, 1)
        for quad in range(4):
            nc.sync.dma_start(
                out=x_planes[32 * quad : 32 * quad + 4, :, :].bitcast(I32),
                in_=x_scales[:, 4 * quad : 4 * quad + 4, :].rearrange("g r n -> r g n").bitcast(I32),
            )
        load_scales(0)
        load_x_codes(1, 3)
        load_codes(0, 1, 3)
        load_x_codes(3, 9)
        load_codes(0, 3, 6)
        load_codes(0, 6, 9)
        load_block(1)
        load_block(2)

        accs = {}
        for batch in range(B):
            for i in range(2):
                acc = psum.tile([P, BANK], F32, name="acc")
                accs[batch, i] = acc
        for cols in bank_slices(NARROW):
            spread_bank(0, rows_a, 2 * D, cols)
        for t in (Q_COLS, K_COLS):
            norm = spread(rows_a[:, t * D : (t + 1) * D])
            for c in range(2):
                nc.vector.scalar_tensor_tensor(
                    out=gains[t][:, c, :].rearrange("p (j i) -> p j i", i=2),
                    in0=rope_in[:].rearrange("p (j i c) -> p j i c", i=2, c=2)[:, :, :, c],
                    scalar=float(D) ** 0.5,
                    in1=norm[:, 0:D].rearrange("p (j c) -> p j c", c=2)[:, :, c : c + 1].to_broadcast([P, D // 2, 2]),
                    op0=ALU.mult,
                    op1=ALU.mult,
                )
        for g in range(PASSES):
            for batch in range(B):
                for i, cols in enumerate(bank_slices(NARROW)):
                    multiply(accs[batch, i], 0, batch, cols, g)
            if g in (4, 5, 6):
                spread_bank(1, rows_b, 0, bank_slices(WIDE)[g - 4])
        for batch in range(B):
            result = work.tile([P, WIDE], F32, name="result", bufs=4)
            for i, cols in enumerate(bank_slices(NARROW)):
                add_bias(result, accs[batch, i], 0, cols)
            store(0, batch, result)

        for n in range(1, len(BLOCKS)):
            if n + 2 < len(BLOCKS):
                load_block(n + 2)
            t, c0, width = BLOCKS[n]
            last = n == len(BLOCKS) - 1
            for batch in range(B):
                if t == V_COLS:
                    dst = work.tile([P, WIDE], F32, name="result", bufs=4)
                else:
                    dst = work.tile([P, WIDE], F32, name="biased")
                for cols in bank_slices(width):
                    acc = psum.tile([P, BANK], F32, name="acc")
                    for g in range(PASSES):
                        multiply(acc, n, batch, cols, g)
                    add_bias(dst, acc, n, cols)
                    if last:
                        store_cols(n, batch, dst, cols)
                if t != V_COLS:
                    dst = norm_and_rope(n, batch, dst)
                if not last:
                    store(n, batch, dst)
